import numpy as np
import ml_dtypes


def mxq(x, axis, fmt="e4m3"):
    dtype, down = {"e4m3": (ml_dtypes.float8_e4m3fn, 7), "e5m2": (ml_dtypes.float8_e5m2, 14)}[fmt]
    v = np.moveaxis(np.asarray(x, np.float32).astype(ml_dtypes.bfloat16).astype(np.float64), axis, -1)
    blocks = v.reshape(v.shape[:-1] + (-1, 32))
    amax = np.abs(blocks).max(-1, keepdims=True)
    byte = np.maximum(np.where(amax > 0, np.frexp(amax)[1] - 1 + 127, 0) - down, 1)
    scale = np.exp2(byte - 127.0)
    codes = (blocks / scale).astype(np.float32).astype(dtype).astype(np.float64)
    return np.moveaxis((codes * scale).reshape(v.shape), -1, axis)


WIDE = False


def mx_kscale(k):
    if not WIDE:
        return np.ones(k)
    levels = np.array([10, -10, 5, -5, 0])
    a = np.random.permutation(np.resize(levels, k // 512 * 4)).reshape(k // 512, 4)
    idx = np.arange(k)
    return np.exp2(a[idx // 512, idx % 128 // 32])


BF16 = ml_dtypes.bfloat16


def bf(x):
    return np.asarray(x, np.float32).astype(BF16)


def f64(x):
    return np.asarray(x).astype(np.float64)


B, S, D, E, WINDOW = 8, 512, 1024, 512, 10
HALF = WINDOW // 2


def setup_inputs():
    s, t = mx_kscale(D), mx_kscale(E)
    return {"x": bf(np.random.standard_normal((B, S, D)) * s),
            "Wq": bf(np.random.standard_normal((E, D)) / np.sqrt(D) / s[None, :] * t[:, None]),
            "bq": bf(np.random.standard_normal(E) * 0.1 * t),
            "k": bf(np.random.standard_normal((B, S, E)) / t)}


def reference(x, Wq, bq, k):
    q = (mxq(f64(x), 2, "e4m3") @ mxq(f64(Wq), 1, "e4m3").T) + f64(bq)
    scores = (mxq(q, 2, "e4m3") @ mxq(f64(k), 2, "e4m3").transpose(0, 2, 1)) / np.sqrt(E)
    i = np.arange(S)[:, None]
    j = np.arange(S)[None, :]
    mask = np.abs(i - j) <= HALF
    scores = np.where(mask[None, :, :], scores, -1e9)
    e = np.exp(scores - scores.max(-1, keepdims=True))
    return e / e.sum(-1, keepdims=True)

@@ -1,0 +1,278 @@
+import math
+from contextlib import ExitStack
+
+import concourse.mybir as mybir
+from concourse.masks import make_identity
+
+F32 = mybir.dt.float32
+BF16 = mybir.dt.bfloat16
+U32 = mybir.dt.uint32
+U8 = mybir.dt.uint8
+I32 = mybir.dt.int32
+FP8X4 = mybir.dt.float8_e4m3fn_x4
+ALU = mybir.AluOpType
+ACT = mybir.ActivationFunctionType
+AXIS = mybir.AxisListType
+
+B, S, D, E, HALF = 8, 512, 1024, 512, 5
+P = 128
+PACK = 4
+K_PASS = P * PACK
+BANK = 512
+R = S // P
+G = D // K_PASS
+WIN = P + 2 * HALF
+K_PAD = 64
+N_SCORES = 2 * P
+WIN_START = K_PAD - HALF
+OUT_PAD = 8
+MASKED = -1.0e9
+
+FLOPS = 2 * B * S * D * E + 2 * B * S * S * E
+
+
+def tile_localattention_pa_t_kernel(tc, x, Wq, bq, k, out):
+    nc = tc.nc
+    with ExitStack() as ctx:
+        const = ctx.enter_context(tc.tile_pool(name="const", bufs=1))
+        inputs = ctx.enter_context(tc.tile_pool(name="inputs", bufs=B))
+        work = ctx.enter_context(tc.tile_pool(name="work", bufs=2))
+        t_psum = ctx.enter_context(tc.psum_pool(name="t_psum", bufs=3))
+        q_psum = ctx.enter_context(tc.psum_pool(name="q_psum", bufs=3))
+        s_psum = ctx.enter_context(tc.psum_pool(name="s_psum", bufs=2))
+
+        w_in = const.tile([P, PACK * D], BF16, name="w_in")
+        nc.sync.dma_start(
+            out=w_in[:].rearrange("c (u ed) -> c u ed", u=2),
+            in_=Wq.rearrange("(u c e) d -> c u (e d)", u=2, e=2),
+        )
+        bias_bf = const.tile([P, PACK], BF16, name="bias_bf")
+        nc.scalar.dma_start(
+            out=bias_bf[:].rearrange("c (u e) -> c u e", u=2),
+            in_=bq.rearrange("(u c e) -> c u e", u=2, e=2),
+        )
+        x_in = {}
+        k_in = {}
+        for b in range(B):
+            x_in[b] = inputs.tile([P, R * D], BF16, name="x_in")
+            nc.sync.dma_start(
+                out=x_in[b][:].rearrange("p (r d) -> p r d", r=R),
+                in_=x[b].rearrange("(r p) d -> p r d", p=P),
+            )
+            k_in[b] = inputs.tile([P, R * E], BF16, name="k_in")
+            nc.sync.dma_start(
+                out=k_in[b][:].rearrange("p (r e) -> p r e", r=R),
+                in_=k[b].rearrange("(r p) e -> p r e", p=P),
+            )
+
+        ident = const.tile([P, P], F32, name="ident")
+        make_identity(nc, ident[:])
+
+        warm = const.tile([P, 1], F32, name="warm")
+        nc.vector.memset(warm[:], 0.0)
+        nc.scalar.activation(out=warm[:], in_=warm[:], func=ACT.Exp)
+
+        bias = const.tile([P, PACK], F32, name="bias")
+        nc.vector.tensor_copy(out=bias[:], in_=bias_bf[:])
+
+        mask = const.tile([P, R, WIN], F32, name="mask")
+        nc.gpsimd.memset(mask[:], 0.0)
+        for r in range(R):
+            nc.gpsimd.affine_select(
+                out=mask[:, r, :], in_=mask[:, r, :], pattern=[[1, WIN]],
+                compare_op=ALU.is_ge, fill=MASKED, base=0, channel_multiplier=-1,
+            )
+            nc.gpsimd.affine_select(
+                out=mask[:, r, :], in_=mask[:, r, :], pattern=[[-1, WIN]],
+                compare_op=ALU.is_ge, fill=MASKED, base=2 * HALF, channel_multiplier=1,
+            )
+        nc.gpsimd.memset(mask[:, 0, 0:HALF], MASKED)
+        nc.gpsimd.memset(mask[:, R - 1, WIN - HALF : WIN], MASKED)
+
+        k_codes = []
+        k_scales = []
+        for n in range(2):
+            k_codes.append(const.tile([P, S + 2 * K_PAD], U32, name="k_codes%d" % n, align_bytes=64))
+            k_scales.append(const.tile([P, S + 2 * K_PAD], U8, name="k_scales%d" % n, align_bytes=64))
+            for pad in (slice(0, K_PAD), slice(K_PAD + S, K_PAD + S + K_PAD)):
+                nc.vector.memset(k_codes[n][:, pad].bitcast(I32), 0)
+                nc.vector.memset(k_scales[n][:, pad].bitcast(I32), 0)
+
+        out_tiles = []
+        for n in range(3):
+            out_tiles.append(const.tile([P, OUT_PAD + R * S + OUT_PAD], F32, name="out_tile%d" % n))
+            nc.vector.memset(out_tiles[n][:], 0.0)
+
+        def regroup_bank(src, dst, n):
+            src_words = src[:].bitcast(F32)
+            dst_words = dst[:].bitcast(F32)
+            bank = t_psum.tile([P, BANK], F32, name="t_bank")
+            for c in range(4):
+                nc.tensor.transpose(
+                    bank[:, P * c : P * (c + 1)],
+                    src_words[:, BANK * n + P * c : BANK * n + P * (c + 1)],
+                    ident[:],
+                )
+            nc.scalar.copy(
+                out=dst_words[:, BANK * n : BANK * (n + 1)].rearrange("p (g w u) -> p g w u", g=2, u=2),
+                in_=bank[:].rearrange("p (g u w) -> p g w u", g=2, u=2),
+            )
+
+        def quantise(grouped, codes, scales):
+            nc.vector.quantize_mx(out=codes.bitcast(FP8X4), scales=scales, in_=grouped)
+
+        x_grouped = {}
+        x_codes = {}
+        x_scales = {}
+        k_grouped = {}
+        q_grouped = {}
+        q_codes = {}
+        q_scales = {}
+        shifted = {}
+        neg_max = {}
+        expd = {}
+        sums = {}
+
+        def new_batch(b):
+            x_grouped[b] = work.tile([P, R * D], BF16, name="x_grouped", align_bytes=64)
+            x_codes[b] = work.tile([P, R * G * P], U32, name="x_codes", align_bytes=64)
+            x_scales[b] = work.tile([P, R * G * P], U8, name="x_scales", align_bytes=64)
+            k_grouped[b] = work.tile([P, S * PACK], BF16, name="k_grouped", align_bytes=64)
+
+        def quantise_x(b, half):
+            quantise(
+                x_grouped[b][:, 2048 * half : 2048 * (half + 1)],
+                x_codes[b][:, 512 * half : 512 * (half + 1)],
+                x_scales[b][:, 512 * half : 512 * (half + 1)],
+            )
+
+        def quantise_k(b):
+            quantise(
+                k_grouped[b][:],
+                k_codes[b % 2][:, K_PAD : K_PAD + S],
+                k_scales[b % 2][:, K_PAD : K_PAD + S],
+            )
+
+        def project(b, r):
+            if r == 0:
+                q_grouped[b] = work.tile([P, S * PACK], BF16, name="q_grouped", align_bytes=64)
+            bank = q_psum.tile([P, BANK], F32, name="q_bank")
+            for t in range(PACK):
+                for g in range(G):
+                    w_cols = slice(P * (G * t + g), P * (G * t + g + 1))
+                    x_cols = slice(P * (G * r + g), P * (G * r + g + 1))
+                    nc.tensor.matmul_mx(
+                        out=bank[:, P * t : P * (t + 1)],
+                        lhsT=w_codes[:, w_cols].bitcast(FP8X4),
+                        lhsT_scale=w_scales[:, w_cols],
+                        rhs=x_codes[b][:, x_cols].bitcast(FP8X4),
+                        rhs_scale=x_scales[b][:, x_cols],
+                        start=(g == 0),
+                        stop=(g == G - 1),
+                    )
+            nc.vector.tensor_tensor(
+                out=q_grouped[b][:, BANK * r : BANK * (r + 1)].rearrange("p (w t) -> p w t", t=PACK),
+                in0=bank[:].rearrange("p (t w) -> p w t", t=PACK),
+                in1=bias[:].unsqueeze(1).to_broadcast([P, P, PACK]),
+                op=ALU.add,
+            )
+
+        def quantise_q(b):
+            q_codes[b] = work.tile([P, S], U32, name="q_codes", align_bytes=64)
+            q_scales[b] = work.tile([P, S], U8, name="q_scales", align_bytes=64)
+            quantise(q_grouped[b][:], q_codes[b][:], q_scales[b][:])
+
+        def scores(b):
+            shifted[b] = work.tile([P, R, WIN], F32, name="shifted")
+            neg_max[b] = work.tile([P, R], F32, name="neg_max")
+            for h in range(R // 2):
+                bank = s_psum.tile([P, BANK], F32, name="s_bank")
+                for n in range(2):
+                    r = 2 * h + n
+                    nc.tensor.matmul_mx(
+                        out=bank[:, N_SCORES * n : N_SCORES * (n + 1)],
+                        lhsT=q_codes[b][:, P * r : P * (r + 1)].bitcast(FP8X4),
+                        lhsT_scale=q_scales[b][:, P * r : P * (r + 1)],
+                        rhs=k_codes[b % 2][:, P * r : P * r + N_SCORES].bitcast(FP8X4),
+                        rhs_scale=k_scales[b % 2][:, P * r : P * r + N_SCORES],
+                        start=True,
+                        stop=True,
+                    )
+                nc.vector.scalar_tensor_tensor(
+                    out=shifted[b][:, 2 * h : 2 * h + 2, :],
+                    in0=bank[:].rearrange("p (n c) -> p n c", n=2)[:, :, WIN_START : WIN_START + WIN],
+                    scalar=1.0 / math.sqrt(E),
+                    in1=mask[:, 2 * h : 2 * h + 2, :],
+                    op0=ALU.mult,
+                    op1=ALU.add,
+                )
+            nc.vector.tensor_reduce(
+                out=neg_max[b][:], in_=shifted[b][:], axis=AXIS.X, op=ALU.max, negate=True
+            )
+
+        def exponentials(b):
+            expd[b] = work.tile([P, R, WIN], F32, name="expd")
+            sums[b] = work.tile([P, R], F32, name="sums")
+            for r in range(R):
+                nc.scalar.activation(
+                    out=expd[b][:, r, :], in_=shifted[b][:, r, :], func=ACT.Exp,
+                    bias=neg_max[b][:, r : r + 1], scale=1.0, accum_out=sums[b][:, r : r + 1],
+                )
+
+        def normalise_and_store(b):
+            inv_sums = work.tile([P, R], F32, name="inv_sums")
+            nc.vector.reciprocal(out=inv_sums[:], in_=sums[b][:])
+            tile = out_tiles[b % 3]
+            for r in range(R):
+                start = OUT_PAD + S * r + P * r - HALF
+                nc.scalar.activation(
+                    out=tile[:, start : start + WIN], in_=expd[b][:, r, :], func=ACT.Copy,
+                    scale=inv_sums[:, r : r + 1],
+                )
+            nc.sync.dma_start(
+                out=out[b].rearrange("(r p) j -> p r j", p=P),
+                in_=tile[:, OUT_PAD : OUT_PAD + R * S].rearrange("p (r j) -> p r j", r=R),
+            )
+
+        w_grouped = const.tile([P, PACK * D], BF16, name="w_grouped", align_bytes=64)
+        w_codes = const.tile([P, PACK * G * P], U32, name="w_codes", align_bytes=64)
+        w_scales = const.tile([P, PACK * G * P], U8, name="w_scales", align_bytes=64)
+        for t in range(PACK):
+            regroup_bank(w_in, w_grouped, t)
+        quantise(w_grouped[:], w_codes[:], w_scales[:])
+
+        new_batch(0)
+        for r in range(R):
+            regroup_bank(x_in[0], x_grouped[0], r)
+        quantise_x(0, 0)
+        quantise_x(0, 1)
+        for n in range(R // 2):
+            regroup_bank(k_in[0], k_grouped[0], n)
+
+        for i in range(B + 1):
+            if i < B:
+                quantise_k(i)
+            if i + 1 < B:
+                new_batch(i + 1)
+                regroup_bank(x_in[i + 1], x_grouped[i + 1], 0)
+                regroup_bank(x_in[i + 1], x_grouped[i + 1], 1)
+                quantise_x(i + 1, 0)
+                regroup_bank(x_in[i + 1], x_grouped[i + 1], 2)
+                regroup_bank(x_in[i + 1], x_grouped[i + 1], 3)
+                regroup_bank(k_in[i + 1], k_grouped[i + 1], 0)
+                regroup_bank(k_in[i + 1], k_grouped[i + 1], 1)
+            if i >= 1:
+                scores(i - 1)
+            if i + 1 < B:
+                quantise_x(i + 1, 1)
+            if i >= 1:
+                exponentials(i - 1)
+            if i < B:
+                project(i, 0)
+                project(i, 1)
+            if i >= 1:
+                normalise_and_store(i - 1)
+            if i < B:
+                project(i, 2)
+                project(i, 3)
+                quantise_q(i)

@@ -40,6 +40,7 @@ def tile_localattention_pa_t_kernel(tc, x, Wq, bq, k, out):
         t_psum = ctx.enter_context(tc.psum_pool(name="t_psum", bufs=3))
         q_psum = ctx.enter_context(tc.psum_pool(name="q_psum", bufs=3))
         s_psum = ctx.enter_context(tc.psum_pool(name="s_psum", bufs=2))
+        ctx.enter_context(tc.manual_schedule())
 
         w_in = const.tile([P, PACK * D], BF16, name="w_in")
         nc.sync.dma_start(
@@ -72,9 +73,6 @@ def tile_localattention_pa_t_kernel(tc, x, Wq, bq, k, out):
         nc.vector.memset(warm[:], 0.0)
         nc.scalar.activation(out=warm[:], in_=warm[:], func=ACT.Exp)
 
-        bias = const.tile([P, PACK], F32, name="bias")
-        nc.vector.tensor_copy(out=bias[:], in_=bias_bf[:])
-
         mask = const.tile([P, R, WIN], F32, name="mask")
         nc.gpsimd.memset(mask[:], 0.0)
         for r in range(R):
@@ -102,6 +100,9 @@ def tile_localattention_pa_t_kernel(tc, x, Wq, bq, k, out):
         for n in range(3):
             out_tiles.append(const.tile([P, OUT_PAD + R * S + OUT_PAD], F32, name="out_tile%d" % n))
             nc.vector.memset(out_tiles[n][:], 0.0)
+
+        bias = const.tile([P, PACK], F32, name="bias")
+        nc.vector.tensor_copy(out=bias[:], in_=bias_bf[:])
 
         def regroup_bank(src, dst, n):
             src_words = src[:].bitcast(F32)

@@ -37,16 +37,15 @@ def tile_localattention_pa_t_kernel(tc, x, Wq, bq, k, out):
         const = ctx.enter_context(tc.tile_pool(name="const", bufs=1))
         inputs = ctx.enter_context(tc.tile_pool(name="inputs", bufs=B))
         work = ctx.enter_context(tc.tile_pool(name="work", bufs=2))
-        t_psum = ctx.enter_context(tc.psum_pool(name="t_psum", bufs=3))
-        q_psum = ctx.enter_context(tc.psum_pool(name="q_psum", bufs=3))
-        s_psum = ctx.enter_context(tc.psum_pool(name="s_psum", bufs=2))
+        psum = ctx.enter_context(tc.psum_pool(name="psum", bufs=8))
         ctx.enter_context(tc.manual_schedule())
 
         w_in = const.tile([P, PACK * D], BF16, name="w_in")
-        nc.sync.dma_start(
-            out=w_in[:].rearrange("c (u ed) -> c u ed", u=2),
-            in_=Wq.rearrange("(u c e) d -> c u (e d)", u=2, e=2),
-        )
+        for u in range(2):
+            nc.sync.dma_start(
+                out=w_in[:, 2 * D * u : 2 * D * (u + 1)],
+                in_=Wq[2 * P * u : 2 * P * (u + 1), :].rearrange("(c e) d -> c (e d)", e=2),
+            )
         bias_bf = const.tile([P, PACK], BF16, name="bias_bf")
         nc.scalar.dma_start(
             out=bias_bf[:].rearrange("c (u e) -> c u e", u=2),
@@ -54,17 +53,26 @@ def tile_localattention_pa_t_kernel(tc, x, Wq, bq, k, out):
         )
         x_in = {}
         k_in = {}
-        for b in range(B):
+
+        def load_x(b):
             x_in[b] = inputs.tile([P, R * D], BF16, name="x_in")
-            nc.sync.dma_start(
-                out=x_in[b][:].rearrange("p (r d) -> p r d", r=R),
-                in_=x[b].rearrange("(r p) d -> p r d", p=P),
-            )
+            for r in range(R):
+                nc.sync.dma_start(out=x_in[b][:, D * r : D * (r + 1)], in_=x[b, P * r : P * (r + 1), :])
+
+        def load_k(b):
             k_in[b] = inputs.tile([P, R * E], BF16, name="k_in")
             nc.sync.dma_start(
                 out=k_in[b][:].rearrange("p (r e) -> p r e", r=R),
                 in_=k[b].rearrange("(r p) e -> p r e", p=P),
             )
+
+        load_x(0)
+        load_k(0)
+        load_x(1)
+        for b in range(2, B):
+            load_x(b)
+            load_k(b - 1)
+        load_k(B - 1)
 
         ident = const.tile([P, P], F32, name="ident")
         make_identity(nc, ident[:])
@@ -97,30 +105,37 @@ def tile_localattention_pa_t_kernel(tc, x, Wq, bq, k, out):
                 nc.vector.memset(k_scales[n][:, pad].bitcast(I32), 0)
 
         out_tiles = []
-        for n in range(3):
+        for n in range(2):
             out_tiles.append(const.tile([P, OUT_PAD + R * S + OUT_PAD], F32, name="out_tile%d" % n))
             nc.vector.memset(out_tiles[n][:], 0.0)
 
         bias = const.tile([P, PACK], F32, name="bias")
         nc.vector.tensor_copy(out=bias[:], in_=bias_bf[:])
 
-        def regroup_bank(src, dst, n):
+        def regroup_bank(src, dst, n, copy):
             src_words = src[:].bitcast(F32)
             dst_words = dst[:].bitcast(F32)
-            bank = t_psum.tile([P, BANK], F32, name="t_bank")
+            bank = psum.tile([P, BANK], F32, name="bank")
             for c in range(4):
                 nc.tensor.transpose(
                     bank[:, P * c : P * (c + 1)],
                     src_words[:, BANK * n + P * c : BANK * n + P * (c + 1)],
                     ident[:],
                 )
-            nc.scalar.copy(
+            copy(
                 out=dst_words[:, BANK * n : BANK * (n + 1)].rearrange("p (g w u) -> p g w u", g=2, u=2),
                 in_=bank[:].rearrange("p (g u w) -> p g w u", g=2, u=2),
             )
 
         def quantise(grouped, codes, scales):
             nc.vector.quantize_mx(out=codes.bitcast(FP8X4), scales=scales, in_=grouped)
+
+        def quantise_half(grouped, codes, scales, half):
+            quantise(
+                grouped[:, 2048 * half : 2048 * (half + 1)],
+                codes[:, 512 * half : 512 * (half + 1)],
+                scales[:, 512 * half : 512 * (half + 1)],
+            )
 
         x_grouped = {}
         x_codes = {}
@@ -133,19 +148,29 @@ def tile_localattention_pa_t_kernel(tc, x, Wq, bq, k, out):
         neg_max = {}
         expd = {}
         sums = {}
+        inv_sums = {}
 
-        def new_batch(b):
+        def new_x(b):
             x_grouped[b] = work.tile([P, R * D], BF16, name="x_grouped", align_bytes=64)
+
+        def new_x_codes(b):
             x_codes[b] = work.tile([P, R * G * P], U32, name="x_codes", align_bytes=64)
             x_scales[b] = work.tile([P, R * G * P], U8, name="x_scales", align_bytes=64)
-            k_grouped[b] = work.tile([P, S * PACK], BF16, name="k_grouped", align_bytes=64)
 
-        def quantise_x(b, half):
-            quantise(
-                x_grouped[b][:, 2048 * half : 2048 * (half + 1)],
-                x_codes[b][:, 512 * half : 512 * (half + 1)],
-                x_scales[b][:, 512 * half : 512 * (half + 1)],
-            )
+        def transpose_x(b):
+            new_x(b)
+            for r in range(R):
+                regroup_bank(x_in[b], x_grouped[b], r, nc.scalar.copy)
+
+        def quantise_x(b):
+            new_x_codes(b)
+            for half in range(2):
+                quantise_half(x_grouped[b], x_codes[b], x_scales[b], half)
+
+        def transpose_k(b):
+            k_grouped[b] = work.tile([P, S * PACK], BF16, name="k_grouped", align_bytes=64)
+            for n in range(R // 2):
+                regroup_bank(k_in[b], k_grouped[b], n, nc.scalar.copy)
 
         def quantise_k(b):
             quantise(
@@ -154,29 +179,29 @@ def tile_localattention_pa_t_kernel(tc, x, Wq, bq, k, out):
                 k_scales[b % 2][:, K_PAD : K_PAD + S],
             )
 
-        def project(b, r):
-            if r == 0:
-                q_grouped[b] = work.tile([P, S * PACK], BF16, name="q_grouped", align_bytes=64)
-            bank = q_psum.tile([P, BANK], F32, name="q_bank")
-            for t in range(PACK):
-                for g in range(G):
-                    w_cols = slice(P * (G * t + g), P * (G * t + g + 1))
-                    x_cols = slice(P * (G * r + g), P * (G * r + g + 1))
-                    nc.tensor.matmul_mx(
-                        out=bank[:, P * t : P * (t + 1)],
-                        lhsT=w_codes[:, w_cols].bitcast(FP8X4),
-                        lhsT_scale=w_scales[:, w_cols],
-                        rhs=x_codes[b][:, x_cols].bitcast(FP8X4),
-                        rhs_scale=x_scales[b][:, x_cols],
-                        start=(g == 0),
-                        stop=(g == G - 1),
-                    )
-            nc.vector.tensor_tensor(
-                out=q_grouped[b][:, BANK * r : BANK * (r + 1)].rearrange("p (w t) -> p w t", t=PACK),
-                in0=bank[:].rearrange("p (t w) -> p w t", t=PACK),
-                in1=bias[:].unsqueeze(1).to_broadcast([P, P, PACK]),
-                op=ALU.add,
-            )
+        def project(b):
+            q_grouped[b] = work.tile([P, S * PACK], BF16, name="q_grouped", align_bytes=64)
+            for r in range(R):
+                bank = psum.tile([P, BANK], F32, name="bank")
+                for t in range(PACK):
+                    for g in range(G):
+                        w_cols = slice(P * (G * t + g), P * (G * t + g + 1))
+                        x_cols = slice(P * (G * r + g), P * (G * r + g + 1))
+                        nc.tensor.matmul_mx(
+                            out=bank[:, P * t : P * (t + 1)],
+                            lhsT=w_codes[:, w_cols].bitcast(FP8X4),
+                            lhsT_scale=w_scales[:, w_cols],
+                            rhs=x_codes[b][:, x_cols].bitcast(FP8X4),
+                            rhs_scale=x_scales[b][:, x_cols],
+                            start=(g == 0),
+                            stop=(g == G - 1),
+                        )
+                nc.vector.tensor_tensor(
+                    out=q_grouped[b][:, BANK * r : BANK * (r + 1)].rearrange("p (w t) -> p w t", t=PACK),
+                    in0=bank[:].rearrange("p (t w) -> p w t", t=PACK),
+                    in1=bias[:].unsqueeze(1).to_broadcast([P, P, PACK]),
+                    op=ALU.add,
+                )
 
         def quantise_q(b):
             q_codes[b] = work.tile([P, S], U32, name="q_codes", align_bytes=64)
@@ -187,7 +212,7 @@ def tile_localattention_pa_t_kernel(tc, x, Wq, bq, k, out):
             shifted[b] = work.tile([P, R, WIN], F32, name="shifted")
             neg_max[b] = work.tile([P, R], F32, name="neg_max")
             for h in range(R // 2):
-                bank = s_psum.tile([P, BANK], F32, name="s_bank")
+                bank = psum.tile([P, BANK], F32, name="bank")
                 for n in range(2):
                     r = 2 * h + n
                     nc.tensor.matmul_mx(
@@ -220,60 +245,53 @@ def tile_localattention_pa_t_kernel(tc, x, Wq, bq, k, out):
                     bias=neg_max[b][:, r : r + 1], scale=1.0, accum_out=sums[b][:, r : r + 1],
                 )
 
-        def normalise_and_store(b):
-            inv_sums = work.tile([P, R], F32, name="inv_sums")
-            nc.vector.reciprocal(out=inv_sums[:], in_=sums[b][:])
-            tile = out_tiles[b % 3]
-            for r in range(R):
-                start = OUT_PAD + S * r + P * r - HALF
-                nc.scalar.activation(
-                    out=tile[:, start : start + WIN], in_=expd[b][:, r, :], func=ACT.Copy,
-                    scale=inv_sums[:, r : r + 1],
-                )
-            nc.sync.dma_start(
-                out=out[b].rearrange("(r p) j -> p r j", p=P),
-                in_=tile[:, OUT_PAD : OUT_PAD + R * S].rearrange("p (r j) -> p r j", r=R),
-            )
+        def invert_sums(b):
+            inv_sums[b] = work.tile([P, R], F32, name="inv_sums")
+            nc.vector.reciprocal(out=inv_sums[b][:], in_=sums[b][:])
 
+        def normalise_and_store(b):
+            tile = out_tiles[b % 2]
+            for r in range(R):
+                row = OUT_PAD + S * r
+                band = row + P * r - HALF
+                nc.scalar.activation(
+                    out=tile[:, band : band + WIN], in_=expd[b][:, r, :], func=ACT.Copy,
+                    scale=inv_sums[b][:, r : r + 1],
+                )
+                nc.sync.dma_start(out=out[b, P * r : P * (r + 1), :], in_=tile[:, row : row + S])
+
+        head_copies = (nc.scalar.copy, nc.vector.tensor_copy)
         w_grouped = const.tile([P, PACK * D], BF16, name="w_grouped", align_bytes=64)
         w_codes = const.tile([P, PACK * G * P], U32, name="w_codes", align_bytes=64)
         w_scales = const.tile([P, PACK * G * P], U8, name="w_scales", align_bytes=64)
-        for t in range(PACK):
-            regroup_bank(w_in, w_grouped, t)
-        quantise(w_grouped[:], w_codes[:], w_scales[:])
+        new_x(0)
+        new_x_codes(0)
+        for src, grouped, codes, scales in (
+            (w_in, w_grouped, w_codes, w_scales),
+            (x_in[0], x_grouped[0], x_codes[0], x_scales[0]),
+        ):
+            for n in range(4):
+                regroup_bank(src, grouped, n, head_copies[n % 2])
+                if n % 2 == 1:
+                    quantise_half(grouped, codes, scales, n // 2)
+        transpose_k(0)
 
-        new_batch(0)
-        for r in range(R):
-            regroup_bank(x_in[0], x_grouped[0], r)
-        quantise_x(0, 0)
-        quantise_x(0, 1)
-        for n in range(R // 2):
-            regroup_bank(k_in[0], k_grouped[0], n)
-
-        for i in range(B + 1):
-            if i < B:
-                quantise_k(i)
-            if i + 1 < B:
-                new_batch(i + 1)
-                regroup_bank(x_in[i + 1], x_grouped[i + 1], 0)
-                regroup_bank(x_in[i + 1], x_grouped[i + 1], 1)
-                quantise_x(i + 1, 0)
-                regroup_bank(x_in[i + 1], x_grouped[i + 1], 2)
-                regroup_bank(x_in[i + 1], x_grouped[i + 1], 3)
-                regroup_bank(k_in[i + 1], k_grouped[i + 1], 0)
-                regroup_bank(k_in[i + 1], k_grouped[i + 1], 1)
+        x_transposed = 1
+        for i in range(B):
+            project(i)
+            quantise_k(i)
+            quantise_q(i)
             if i >= 1:
-                scores(i - 1)
+                invert_sums(i - 1)
+            for b in range(x_transposed, min(i + 3, B)):
+                transpose_x(b)
+            x_transposed = min(i + 3, B)
             if i + 1 < B:
-                quantise_x(i + 1, 1)
-            if i >= 1:
-                exponentials(i - 1)
-            if i < B:
-                project(i, 0)
-                project(i, 1)
+                transpose_k(i + 1)
+                quantise_x(i + 1)
+            scores(i)
             if i >= 1:
                 normalise_and_store(i - 1)
-            if i < B:
-                project(i, 2)
-                project(i, 3)
-                quantise_q(i)
+            exponentials(i)
+        invert_sums(B - 1)
+        normalise_and_store(B - 1)

@@ -27,6 +27,7 @@ N_SCORES = 2 * P
 WIN_START = K_PAD - HALF
 OUT_PAD = 8
 MASKED = -1.0e9
+SHARED_BATCHES = 2
 
 FLOPS = 2 * B * S * D * E + 2 * B * S * S * E
 
@@ -127,6 +128,11 @@ def tile_localattention_pa_t_kernel(tc, x, Wq, bq, k, out):
                 in_=bank[:].rearrange("p (g u w) -> p g w u", g=2, u=2),
             )
 
+        def bank_copy(shared, n):
+            if shared and n % 2 == 1:
+                return nc.vector.tensor_copy
+            return nc.scalar.copy
+
         def quantise(grouped, codes, scales):
             nc.vector.quantize_mx(out=codes.bitcast(FP8X4), scales=scales, in_=grouped)
 
@@ -160,7 +166,7 @@ def tile_localattention_pa_t_kernel(tc, x, Wq, bq, k, out):
         def transpose_x(b):
             new_x(b)
             for r in range(R):
-                regroup_bank(x_in[b], x_grouped[b], r, nc.scalar.copy)
+                regroup_bank(x_in[b], x_grouped[b], r, bank_copy(b < SHARED_BATCHES, r))
 
         def quantise_x(b):
             new_x_codes(b)
@@ -179,8 +185,15 @@ def tile_localattention_pa_t_kernel(tc, x, Wq, bq, k, out):
                 k_scales[b % 2][:, K_PAD : K_PAD + S],
             )
 
-        def project(b):
+        def piece(b):
+            if b == B - 1:
+                return R // 2
+            return R
+
+        def project_and_quantise(b):
             q_grouped[b] = work.tile([P, S * PACK], BF16, name="q_grouped", align_bytes=64)
+            q_codes[b] = work.tile([P, S], U32, name="q_codes", align_bytes=64)
+            q_scales[b] = work.tile([P, S], U8, name="q_scales", align_bytes=64)
             for r in range(R):
                 bank = psum.tile([P, BANK], F32, name="bank")
                 for t in range(PACK):
@@ -202,11 +215,13 @@ def tile_localattention_pa_t_kernel(tc, x, Wq, bq, k, out):
                     in1=bias[:].unsqueeze(1).to_broadcast([P, P, PACK]),
                     op=ALU.add,
                 )
-
-        def quantise_q(b):
-            q_codes[b] = work.tile([P, S], U32, name="q_codes", align_bytes=64)
-            q_scales[b] = work.tile([P, S], U8, name="q_scales", align_bytes=64)
-            quantise(q_grouped[b][:], q_codes[b][:], q_scales[b][:])
+                if (r + 1) % piece(b) == 0:
+                    first = r + 1 - piece(b)
+                    quantise(
+                        q_grouped[b][:, BANK * first : BANK * (r + 1)],
+                        q_codes[b][:, P * first : P * (r + 1)],
+                        q_scales[b][:, P * first : P * (r + 1)],
+                    )
 
         def scores(b):
             shifted[b] = work.tile([P, R, WIN], F32, name="shifted")
@@ -232,9 +247,12 @@ def tile_localattention_pa_t_kernel(tc, x, Wq, bq, k, out):
                     op0=ALU.mult,
                     op1=ALU.add,
                 )
-            nc.vector.tensor_reduce(
-                out=neg_max[b][:], in_=shifted[b][:], axis=AXIS.X, op=ALU.max, negate=True
-            )
+                if (2 * h + 2) % piece(b) == 0:
+                    tiles = slice(2 * h + 2 - piece(b), 2 * h + 2)
+                    nc.vector.tensor_reduce(
+                        out=neg_max[b][:, tiles], in_=shifted[b][:, tiles, :],
+                        axis=AXIS.X, op=ALU.max, negate=True,
+                    )
 
         def exponentials(b):
             expd[b] = work.tile([P, R, WIN], F32, name="expd")
@@ -247,7 +265,9 @@ def tile_localattention_pa_t_kernel(tc, x, Wq, bq, k, out):
 
         def invert_sums(b):
             inv_sums[b] = work.tile([P, R], F32, name="inv_sums")
-            nc.vector.reciprocal(out=inv_sums[b][:], in_=sums[b][:])
+            for first in range(0, R, piece(b)):
+                tiles = slice(first, first + piece(b))
+                nc.vector.reciprocal(out=inv_sums[b][:, tiles], in_=sums[b][:, tiles])
 
         def normalise_and_store(b):
             tile = out_tiles[b % 2]
@@ -260,7 +280,6 @@ def tile_localattention_pa_t_kernel(tc, x, Wq, bq, k, out):
                 )
                 nc.sync.dma_start(out=out[b, P * r : P * (r + 1), :], in_=tile[:, row : row + S])
 
-        head_copies = (nc.scalar.copy, nc.vector.tensor_copy)
         w_grouped = const.tile([P, PACK * D], BF16, name="w_grouped", align_bytes=64)
         w_codes = const.tile([P, PACK * G * P], U32, name="w_codes", align_bytes=64)
         w_scales = const.tile([P, PACK * G * P], U8, name="w_scales", align_bytes=64)
@@ -271,16 +290,15 @@ def tile_localattention_pa_t_kernel(tc, x, Wq, bq, k, out):
             (x_in[0], x_grouped[0], x_codes[0], x_scales[0]),
         ):
             for n in range(4):
-                regroup_bank(src, grouped, n, head_copies[n % 2])
+                regroup_bank(src, grouped, n, bank_copy(True, n))
                 if n % 2 == 1:
                     quantise_half(grouped, codes, scales, n // 2)
         transpose_k(0)
+        project_and_quantise(0)
+        quantise_k(0)
 
         x_transposed = 1
         for i in range(B):
-            project(i)
-            quantise_k(i)
-            quantise_q(i)
             if i >= 1:
                 invert_sums(i - 1)
             for b in range(x_transposed, min(i + 3, B)):
@@ -290,8 +308,12 @@ def tile_localattention_pa_t_kernel(tc, x, Wq, bq, k, out):
                 transpose_k(i + 1)
                 quantise_x(i + 1)
             scores(i)
+            if i + 1 < B:
+                quantise_k(i + 1)
             if i >= 1:
                 normalise_and_store(i - 1)
             exponentials(i)
+            if i + 1 < B:
+                project_and_quantise(i + 1)
         invert_sums(B - 1)
         normalise_and_store(B - 1)

@@ -27,7 +27,7 @@ N_SCORES = 2 * P
 WIN_START = K_PAD - HALF
 OUT_PAD = 8
 MASKED = -1.0e9
-SHARED_BATCHES = 2
+SHARED_BATCHES = 1
 
 FLOPS = 2 * B * S * D * E + 2 * B * S * S * E
 
@@ -129,7 +129,7 @@ def tile_localattention_pa_t_kernel(tc, x, Wq, bq, k, out):
             )
 
         def bank_copy(shared, n):
-            if shared and n % 2 == 1:
+            if shared and n % 2 == 0:
                 return nc.vector.tensor_copy
             return nc.scalar.copy
 
@@ -185,10 +185,12 @@ def tile_localattention_pa_t_kernel(tc, x, Wq, bq, k, out):
                 k_scales[b % 2][:, K_PAD : K_PAD + S],
             )
 
-        def piece(b):
-            if b == B - 1:
-                return R // 2
-            return R
+        def quantise_q(b, half):
+            quantise(
+                q_grouped[b][:, 1024 * half : 1024 * (half + 1)],
+                q_codes[b][:, 256 * half : 256 * (half + 1)],
+                q_scales[b][:, 256 * half : 256 * (half + 1)],
+            )
 
         def project_and_quantise(b):
             q_grouped[b] = work.tile([P, S * PACK], BF16, name="q_grouped", align_bytes=64)
@@ -215,13 +217,10 @@ def tile_localattention_pa_t_kernel(tc, x, Wq, bq, k, out):
                     in1=bias[:].unsqueeze(1).to_broadcast([P, P, PACK]),
                     op=ALU.add,
                 )
-                if (r + 1) % piece(b) == 0:
-                    first = r + 1 - piece(b)
-                    quantise(
-                        q_grouped[b][:, BANK * first : BANK * (r + 1)],
-                        q_codes[b][:, P * first : P * (r + 1)],
-                        q_scales[b][:, P * first : P * (r + 1)],
-                    )
+                if r == R // 2:
+                    quantise_q(b, 0)
+            quantise_k(b)
+            quantise_q(b, 1)
 
         def scores(b):
             shifted[b] = work.tile([P, R, WIN], F32, name="shifted")
@@ -247,12 +246,12 @@ def tile_localattention_pa_t_kernel(tc, x, Wq, bq, k, out):
                     op0=ALU.mult,
                     op1=ALU.add,
                 )
-                if (2 * h + 2) % piece(b) == 0:
-                    tiles = slice(2 * h + 2 - piece(b), 2 * h + 2)
-                    nc.vector.tensor_reduce(
-                        out=neg_max[b][:, tiles], in_=shifted[b][:, tiles, :],
-                        axis=AXIS.X, op=ALU.max, negate=True,
-                    )
+            for h in range(R // 2):
+                tiles = slice(2 * h, 2 * h + 2)
+                nc.vector.tensor_reduce(
+                    out=neg_max[b][:, tiles], in_=shifted[b][:, tiles, :],
+                    axis=AXIS.X, op=ALU.max, negate=True,
+                )
 
         def exponentials(b):
             expd[b] = work.tile([P, R, WIN], F32, name="expd")
@@ -265,9 +264,7 @@ def tile_localattention_pa_t_kernel(tc, x, Wq, bq, k, out):
 
         def invert_sums(b):
             inv_sums[b] = work.tile([P, R], F32, name="inv_sums")
-            for first in range(0, R, piece(b)):
-                tiles = slice(first, first + piece(b))
-                nc.vector.reciprocal(out=inv_sums[b][:, tiles], in_=sums[b][:, tiles])
+            nc.vector.reciprocal(out=inv_sums[b][:], in_=sums[b][:])
 
         def normalise_and_store(b):
             tile = out_tiles[b % 2]
@@ -295,7 +292,6 @@ def tile_localattention_pa_t_kernel(tc, x, Wq, bq, k, out):
                     quantise_half(grouped, codes, scales, n // 2)
         transpose_k(0)
         project_and_quantise(0)
-        quantise_k(0)
 
         x_transposed = 1
         for i in range(B):
@@ -308,8 +304,6 @@ def tile_localattention_pa_t_kernel(tc, x, Wq, bq, k, out):
                 transpose_k(i + 1)
                 quantise_x(i + 1)
             scores(i)
-            if i + 1 < B:
-                quantise_k(i + 1)
             if i >= 1:
                 normalise_and_store(i - 1)
             exponentials(i)

@@ -39,7 +39,6 @@ def tile_localattention_pa_t_kernel(tc, x, Wq, bq, k, out):
         inputs = ctx.enter_context(tc.tile_pool(name="inputs", bufs=B))
         work = ctx.enter_context(tc.tile_pool(name="work", bufs=2))
         psum = ctx.enter_context(tc.psum_pool(name="psum", bufs=8))
-        ctx.enter_context(tc.manual_schedule())
 
         w_in = const.tile([P, PACK * D], BF16, name="w_in")
         for u in range(2):

@@ -14,20 +14,24 @@ ALU = mybir.AluOpType
 ACT = mybir.ActivationFunctionType
 AXIS = mybir.AxisListType
 
-B, S, D, E, HALF = 8, 512, 1024, 512, 5
+B, S, D, E = 8, 512, 1024, 512
+HALF = 5
 P = 128
 PACK = 4
 K_PASS = P * PACK
 BANK = 512
+BANK_VALUES = 2 * BANK
 R = S // P
 G = D // K_PASS
+W_BANKS = PACK * D // BANK_VALUES
 WIN = P + 2 * HALF
 K_PAD = 64
 N_SCORES = 2 * P
 WIN_START = K_PAD - HALF
 OUT_PAD = 8
+OUT_HOMES = 3
+X_LEAD = 2
 MASKED = -1.0e9
-SHARED_BATCHES = 1
 
 FLOPS = 2 * B * S * D * E + 2 * B * S * S * E
 
@@ -39,6 +43,7 @@ def tile_localattention_pa_t_kernel(tc, x, Wq, bq, k, out):
         inputs = ctx.enter_context(tc.tile_pool(name="inputs", bufs=B))
         work = ctx.enter_context(tc.tile_pool(name="work", bufs=2))
         psum = ctx.enter_context(tc.psum_pool(name="psum", bufs=8))
+        ctx.enter_context(tc.manual_schedule())
 
         w_in = const.tile([P, PACK * D], BF16, name="w_in")
         for u in range(2):
@@ -62,17 +67,13 @@ def tile_localattention_pa_t_kernel(tc, x, Wq, bq, k, out):
         def load_k(b):
             k_in[b] = inputs.tile([P, R * E], BF16, name="k_in")
             nc.sync.dma_start(
-                out=k_in[b][:].rearrange("p (r e) -> p r e", r=R),
-                in_=k[b].rearrange("(r p) e -> p r e", p=P),
+                out=k_in[b][:].rearrange("p (r f) -> p r f", r=R),
+                in_=k[b].rearrange("(r p) f -> p r f", p=P),
             )
 
-        load_x(0)
-        load_k(0)
-        load_x(1)
-        for b in range(2, B):
+        for b in range(B):
             load_x(b)
-            load_k(b - 1)
-        load_k(B - 1)
+            load_k(b)
 
         ident = const.tile([P, P], F32, name="ident")
         make_identity(nc, ident[:])
@@ -97,50 +98,43 @@ def tile_localattention_pa_t_kernel(tc, x, Wq, bq, k, out):
 
         k_codes = []
         k_scales = []
-        for n in range(2):
-            k_codes.append(const.tile([P, S + 2 * K_PAD], U32, name="k_codes%d" % n, align_bytes=64))
-            k_scales.append(const.tile([P, S + 2 * K_PAD], U8, name="k_scales%d" % n, align_bytes=64))
+        for home in range(2):
+            k_codes.append(const.tile([P, S + 2 * K_PAD], U32, name="k_codes%d" % home, align_bytes=64))
+            k_scales.append(const.tile([P, S + 2 * K_PAD], U8, name="k_scales%d" % home, align_bytes=64))
             for pad in (slice(0, K_PAD), slice(K_PAD + S, K_PAD + S + K_PAD)):
-                nc.vector.memset(k_codes[n][:, pad].bitcast(I32), 0)
-                nc.vector.memset(k_scales[n][:, pad].bitcast(I32), 0)
+                nc.vector.memset(k_codes[home][:, pad].bitcast(I32), 0)
+                nc.vector.memset(k_scales[home][:, pad].bitcast(I32), 0)
 
         out_tiles = []
-        for n in range(2):
-            out_tiles.append(const.tile([P, OUT_PAD + R * S + OUT_PAD], F32, name="out_tile%d" % n))
-            nc.vector.memset(out_tiles[n][:], 0.0)
+        for home in range(OUT_HOMES):
+            out_tiles.append(const.tile([P, OUT_PAD + R * S + OUT_PAD], F32, name="out_tile%d" % home))
+            nc.vector.memset(out_tiles[home][:], 0.0)
 
         bias = const.tile([P, PACK], F32, name="bias")
         nc.vector.tensor_copy(out=bias[:], in_=bias_bf[:])
 
         def regroup_bank(src, dst, n, copy):
-            src_words = src[:].bitcast(F32)
-            dst_words = dst[:].bitcast(F32)
+            src_pairs = src[:].bitcast(F32)
+            dst_pairs = dst[:].bitcast(F32)
             bank = psum.tile([P, BANK], F32, name="bank")
-            for c in range(4):
+            for piece in range(BANK // P):
                 nc.tensor.transpose(
-                    bank[:, P * c : P * (c + 1)],
-                    src_words[:, BANK * n + P * c : BANK * n + P * (c + 1)],
+                    bank[:, P * piece : P * (piece + 1)],
+                    src_pairs[:, BANK * n + P * piece : BANK * n + P * (piece + 1)],
                     ident[:],
                 )
             copy(
-                out=dst_words[:, BANK * n : BANK * (n + 1)].rearrange("p (g w u) -> p g w u", g=2, u=2),
-                in_=bank[:].rearrange("p (g u w) -> p g w u", g=2, u=2),
+                out=dst_pairs[:, BANK * n : BANK * (n + 1)].rearrange("c (g w u) -> c g w u", g=2, u=2),
+                in_=bank[:].rearrange("c (g u w) -> c g w u", g=2, u=2),
             )
-
-        def bank_copy(shared, n):
-            if shared and n % 2 == 0:
-                return nc.vector.tensor_copy
-            return nc.scalar.copy
 
         def quantise(grouped, codes, scales):
             nc.vector.quantize_mx(out=codes.bitcast(FP8X4), scales=scales, in_=grouped)
 
-        def quantise_half(grouped, codes, scales, half):
-            quantise(
-                grouped[:, 2048 * half : 2048 * (half + 1)],
-                codes[:, 512 * half : 512 * (half + 1)],
-                scales[:, 512 * half : 512 * (half + 1)],
-            )
+        def quantise_two_banks(grouped, codes, scales, part):
+            values = slice(2 * BANK_VALUES * part, 2 * BANK_VALUES * (part + 1))
+            words = slice(2 * BANK_VALUES // PACK * part, 2 * BANK_VALUES // PACK * (part + 1))
+            quantise(grouped[:, values], codes[:, words], scales[:, words])
 
         x_grouped = {}
         x_codes = {}
@@ -165,12 +159,12 @@ def tile_localattention_pa_t_kernel(tc, x, Wq, bq, k, out):
         def transpose_x(b):
             new_x(b)
             for r in range(R):
-                regroup_bank(x_in[b], x_grouped[b], r, bank_copy(b < SHARED_BATCHES, r))
+                regroup_bank(x_in[b], x_grouped[b], r, nc.scalar.copy)
 
         def quantise_x(b):
             new_x_codes(b)
-            for half in range(2):
-                quantise_half(x_grouped[b], x_codes[b], x_scales[b], half)
+            for part in range(2):
+                quantise_two_banks(x_grouped[b], x_codes[b], x_scales[b], part)
 
         def transpose_k(b):
             k_grouped[b] = work.tile([P, S * PACK], BF16, name="k_grouped", align_bytes=64)
@@ -184,12 +178,10 @@ def tile_localattention_pa_t_kernel(tc, x, Wq, bq, k, out):
                 k_scales[b % 2][:, K_PAD : K_PAD + S],
             )
 
-        def quantise_q(b, half):
-            quantise(
-                q_grouped[b][:, 1024 * half : 1024 * (half + 1)],
-                q_codes[b][:, 256 * half : 256 * (half + 1)],
-                q_scales[b][:, 256 * half : 256 * (half + 1)],
-            )
+        def quantise_q(b, part):
+            tokens = slice(2 * P * part, 2 * P * (part + 1))
+            values = slice(2 * P * PACK * part, 2 * P * PACK * (part + 1))
+            quantise(q_grouped[b][:, values], q_codes[b][:, tokens], q_scales[b][:, tokens])
 
         def project_and_quantise(b):
             q_grouped[b] = work.tile([P, S * PACK], BF16, name="q_grouped", align_bytes=64)
@@ -211,8 +203,8 @@ def tile_localattention_pa_t_kernel(tc, x, Wq, bq, k, out):
                             stop=(g == G - 1),
                         )
                 nc.vector.tensor_tensor(
-                    out=q_grouped[b][:, BANK * r : BANK * (r + 1)].rearrange("p (w t) -> p w t", t=PACK),
-                    in0=bank[:].rearrange("p (t w) -> p w t", t=PACK),
+                    out=q_grouped[b][:, BANK * r : BANK * (r + 1)].rearrange("c (w t) -> c w t", t=PACK),
+                    in0=bank[:].rearrange("c (t w) -> c w t", t=PACK),
                     in1=bias[:].unsqueeze(1).to_broadcast([P, P, PACK]),
                     op=ALU.add,
                 )
@@ -224,12 +216,12 @@ def tile_localattention_pa_t_kernel(tc, x, Wq, bq, k, out):
         def scores(b):
             shifted[b] = work.tile([P, R, WIN], F32, name="shifted")
             neg_max[b] = work.tile([P, R], F32, name="neg_max")
-            for h in range(R // 2):
+            for pair in range(R // 2):
                 bank = psum.tile([P, BANK], F32, name="bank")
-                for n in range(2):
-                    r = 2 * h + n
+                for side in range(2):
+                    r = 2 * pair + side
                     nc.tensor.matmul_mx(
-                        out=bank[:, N_SCORES * n : N_SCORES * (n + 1)],
+                        out=bank[:, N_SCORES * side : N_SCORES * (side + 1)],
                         lhsT=q_codes[b][:, P * r : P * (r + 1)].bitcast(FP8X4),
                         lhsT_scale=q_scales[b][:, P * r : P * (r + 1)],
                         rhs=k_codes[b % 2][:, P * r : P * r + N_SCORES].bitcast(FP8X4),
@@ -238,17 +230,16 @@ def tile_localattention_pa_t_kernel(tc, x, Wq, bq, k, out):
                         stop=True,
                     )
                 nc.vector.scalar_tensor_tensor(
-                    out=shifted[b][:, 2 * h : 2 * h + 2, :],
-                    in0=bank[:].rearrange("p (n c) -> p n c", n=2)[:, :, WIN_START : WIN_START + WIN],
+                    out=shifted[b][:, 2 * pair : 2 * pair + 2, :],
+                    in0=bank[:].rearrange("p (side v) -> p side v", side=2)[:, :, WIN_START : WIN_START + WIN],
                     scalar=1.0 / math.sqrt(E),
-                    in1=mask[:, 2 * h : 2 * h + 2, :],
+                    in1=mask[:, 2 * pair : 2 * pair + 2, :],
                     op0=ALU.mult,
                     op1=ALU.add,
                 )
-            for h in range(R // 2):
-                tiles = slice(2 * h, 2 * h + 2)
+            for pair in range(R // 2):
                 nc.vector.tensor_reduce(
-                    out=neg_max[b][:, tiles], in_=shifted[b][:, tiles, :],
+                    out=neg_max[b][:, 2 * pair : 2 * pair + 2], in_=shifted[b][:, 2 * pair : 2 * pair + 2, :],
                     axis=AXIS.X, op=ALU.max, negate=True,
                 )
 
@@ -266,29 +257,31 @@ def tile_localattention_pa_t_kernel(tc, x, Wq, bq, k, out):
             nc.vector.reciprocal(out=inv_sums[b][:], in_=sums[b][:])
 
         def normalise_and_store(b):
-            tile = out_tiles[b % 2]
             for r in range(R):
                 row = OUT_PAD + S * r
                 band = row + P * r - HALF
                 nc.scalar.activation(
-                    out=tile[:, band : band + WIN], in_=expd[b][:, r, :], func=ACT.Copy,
+                    out=out_tiles[b % OUT_HOMES][:, band : band + WIN], in_=expd[b][:, r, :], func=ACT.Copy,
                     scale=inv_sums[b][:, r : r + 1],
                 )
-                nc.sync.dma_start(out=out[b, P * r : P * (r + 1), :], in_=tile[:, row : row + S])
+                nc.sync.dma_start(
+                    out=out[b, P * r : P * (r + 1), :], in_=out_tiles[b % OUT_HOMES][:, row : row + S]
+                )
 
         w_grouped = const.tile([P, PACK * D], BF16, name="w_grouped", align_bytes=64)
         w_codes = const.tile([P, PACK * G * P], U32, name="w_codes", align_bytes=64)
         w_scales = const.tile([P, PACK * G * P], U8, name="w_scales", align_bytes=64)
         new_x(0)
         new_x_codes(0)
+        head_copies = (nc.vector.tensor_copy, nc.scalar.copy)
         for src, grouped, codes, scales in (
             (w_in, w_grouped, w_codes, w_scales),
             (x_in[0], x_grouped[0], x_codes[0], x_scales[0]),
         ):
-            for n in range(4):
-                regroup_bank(src, grouped, n, bank_copy(True, n))
+            for n in range(W_BANKS):
+                regroup_bank(src, grouped, n, head_copies[n % 2])
                 if n % 2 == 1:
-                    quantise_half(grouped, codes, scales, n // 2)
+                    quantise_two_banks(grouped, codes, scales, n // 2)
         transpose_k(0)
         project_and_quantise(0)
 
@@ -296,9 +289,10 @@ def tile_localattention_pa_t_kernel(tc, x, Wq, bq, k, out):
         for i in range(B):
             if i >= 1:
                 invert_sums(i - 1)
-            for b in range(x_transposed, min(i + 3, B)):
+            x_wanted = min(i + 1 + min(i + 1, X_LEAD), B)
+            for b in range(x_transposed, x_wanted):
                 transpose_x(b)
-            x_transposed = min(i + 3, B)
+            x_transposed = x_wanted
             if i + 1 < B:
                 transpose_k(i + 1)
                 quantise_x(i + 1)

import math
from contextlib import ExitStack

import concourse.mybir as mybir
from concourse.masks import make_identity

F32 = mybir.dt.float32
BF16 = mybir.dt.bfloat16
U32 = mybir.dt.uint32
U8 = mybir.dt.uint8
I32 = mybir.dt.int32
FP8X4 = mybir.dt.float8_e4m3fn_x4
ALU = mybir.AluOpType
ACT = mybir.ActivationFunctionType
AXIS = mybir.AxisListType

B, S, D, E = 8, 512, 1024, 512
HALF = 5
P = 128
PACK = 4
K_PASS = P * PACK
BANK = 512
BANK_VALUES = 2 * BANK
R = S // P
G = D // K_PASS
W_BANKS = PACK * D // BANK_VALUES
WIN = P + 2 * HALF
K_PAD = 64
N_SCORES = 2 * P
WIN_START = K_PAD - HALF
OUT_PAD = 8
OUT_HOMES = 3
X_LEAD = 2
MASKED = -1.0e9

FLOPS = 2 * B * S * D * E + 2 * B * S * S * E


def tile_localattention_pa_t_kernel(tc, x, Wq, bq, k, out):
    nc = tc.nc
    with ExitStack() as ctx:
        const = ctx.enter_context(tc.tile_pool(name="const", bufs=1))
        inputs = ctx.enter_context(tc.tile_pool(name="inputs", bufs=B))
        work = ctx.enter_context(tc.tile_pool(name="work", bufs=2))
        psum = ctx.enter_context(tc.psum_pool(name="psum", bufs=8))
        ctx.enter_context(tc.manual_schedule())

        w_in = const.tile([P, PACK * D], BF16, name="w_in")
        for u in range(2):
            nc.sync.dma_start(
                out=w_in[:, 2 * D * u : 2 * D * (u + 1)],
                in_=Wq[2 * P * u : 2 * P * (u + 1), :].rearrange("(c e) d -> c (e d)", e=2),
            )
        bias_bf = const.tile([P, PACK], BF16, name="bias_bf")
        nc.scalar.dma_start(
            out=bias_bf[:].rearrange("c (u e) -> c u e", u=2),
            in_=bq.rearrange("(u c e) -> c u e", u=2, e=2),
        )
        x_in = {}
        k_in = {}

        def load_x(b):
            x_in[b] = inputs.tile([P, R * D], BF16, name="x_in")
            for r in range(R):
                nc.sync.dma_start(out=x_in[b][:, D * r : D * (r + 1)], in_=x[b, P * r : P * (r + 1), :])

        def load_k(b):
            k_in[b] = inputs.tile([P, R * E], BF16, name="k_in")
            nc.sync.dma_start(
                out=k_in[b][:].rearrange("p (r f) -> p r f", r=R),
                in_=k[b].rearrange("(r p) f -> p r f", p=P),
            )

        for b in range(B):
            load_x(b)
            load_k(b)

        ident = const.tile([P, P], F32, name="ident")
        make_identity(nc, ident[:])

        warm = const.tile([P, 1], F32, name="warm")
        nc.vector.memset(warm[:], 0.0)
        nc.scalar.activation(out=warm[:], in_=warm[:], func=ACT.Exp)

        mask = const.tile([P, R, WIN], F32, name="mask")
        nc.gpsimd.memset(mask[:], 0.0)
        for r in range(R):
            nc.gpsimd.affine_select(
                out=mask[:, r, :], in_=mask[:, r, :], pattern=[[1, WIN]],
                compare_op=ALU.is_ge, fill=MASKED, base=0, channel_multiplier=-1,
            )
            nc.gpsimd.affine_select(
                out=mask[:, r, :], in_=mask[:, r, :], pattern=[[-1, WIN]],
                compare_op=ALU.is_ge, fill=MASKED, base=2 * HALF, channel_multiplier=1,
            )
        nc.gpsimd.memset(mask[:, 0, 0:HALF], MASKED)
        nc.gpsimd.memset(mask[:, R - 1, WIN - HALF : WIN], MASKED)

        k_codes = []
        k_scales = []
        for home in range(2):
            k_codes.append(const.tile([P, S + 2 * K_PAD], U32, name="k_codes%d" % home, align_bytes=64))
            k_scales.append(const.tile([P, S + 2 * K_PAD], U8, name="k_scales%d" % home, align_bytes=64))
            for pad in (slice(0, K_PAD), slice(K_PAD + S, K_PAD + S + K_PAD)):
                nc.vector.memset(k_codes[home][:, pad].bitcast(I32), 0)
                nc.vector.memset(k_scales[home][:, pad].bitcast(I32), 0)

        out_tiles = []
        for home in range(OUT_HOMES):
            out_tiles.append(const.tile([P, OUT_PAD + R * S + OUT_PAD], F32, name="out_tile%d" % home))
            nc.vector.memset(out_tiles[home][:], 0.0)

        bias = const.tile([P, PACK], F32, name="bias")
        nc.vector.tensor_copy(out=bias[:], in_=bias_bf[:])

        def regroup_bank(src, dst, n, copy):
            src_pairs = src[:].bitcast(F32)
            dst_pairs = dst[:].bitcast(F32)
            bank = psum.tile([P, BANK], F32, name="bank")
            for piece in range(BANK // P):
                nc.tensor.transpose(
                    bank[:, P * piece : P * (piece + 1)],
                    src_pairs[:, BANK * n + P * piece : BANK * n + P * (piece + 1)],
                    ident[:],
                )
            copy(
                out=dst_pairs[:, BANK * n : BANK * (n + 1)].rearrange("c (g w u) -> c g w u", g=2, u=2),
                in_=bank[:].rearrange("c (g u w) -> c g w u", g=2, u=2),
            )

        def quantise(grouped, codes, scales):
            nc.vector.quantize_mx(out=codes.bitcast(FP8X4), scales=scales, in_=grouped)

        def quantise_two_banks(grouped, codes, scales, part):
            values = slice(2 * BANK_VALUES * part, 2 * BANK_VALUES * (part + 1))
            words = slice(2 * BANK_VALUES // PACK * part, 2 * BANK_VALUES // PACK * (part + 1))
            quantise(grouped[:, values], codes[:, words], scales[:, words])

        x_grouped = {}
        x_codes = {}
        x_scales = {}
        k_grouped = {}
        q_grouped = {}
        q_codes = {}
        q_scales = {}
        shifted = {}
        neg_max = {}
        expd = {}
        sums = {}
        inv_sums = {}

        def new_x(b):
            x_grouped[b] = work.tile([P, R * D], BF16, name="x_grouped", align_bytes=64)

        def new_x_codes(b):
            x_codes[b] = work.tile([P, R * G * P], U32, name="x_codes", align_bytes=64)
            x_scales[b] = work.tile([P, R * G * P], U8, name="x_scales", align_bytes=64)

        def transpose_x(b):
            new_x(b)
            for r in range(R):
                regroup_bank(x_in[b], x_grouped[b], r, nc.scalar.copy)

        def quantise_x(b):
            new_x_codes(b)
            for part in range(2):
                quantise_two_banks(x_grouped[b], x_codes[b], x_scales[b], part)

        def transpose_k(b):
            k_grouped[b] = work.tile([P, S * PACK], BF16, name="k_grouped", align_bytes=64)
            for n in range(R // 2):
                regroup_bank(k_in[b], k_grouped[b], n, nc.scalar.copy)

        def quantise_k(b):
            quantise(
                k_grouped[b][:],
                k_codes[b % 2][:, K_PAD : K_PAD + S],
                k_scales[b % 2][:, K_PAD : K_PAD + S],
            )

        def quantise_q(b, part):
            tokens = slice(2 * P * part, 2 * P * (part + 1))
            values = slice(2 * P * PACK * part, 2 * P * PACK * (part + 1))
            quantise(q_grouped[b][:, values], q_codes[b][:, tokens], q_scales[b][:, tokens])

        def project_and_quantise(b):
            q_grouped[b] = work.tile([P, S * PACK], BF16, name="q_grouped", align_bytes=64)
            q_codes[b] = work.tile([P, S], U32, name="q_codes", align_bytes=64)
            q_scales[b] = work.tile([P, S], U8, name="q_scales", align_bytes=64)
            for r in range(R):
                bank = psum.tile([P, BANK], F32, name="bank")
                for t in range(PACK):
                    for g in range(G):
                        w_cols = slice(P * (G * t + g), P * (G * t + g + 1))
                        x_cols = slice(P * (G * r + g), P * (G * r + g + 1))
                        nc.tensor.matmul_mx(
                            out=bank[:, P * t : P * (t + 1)],
                            lhsT=w_codes[:, w_cols].bitcast(FP8X4),
                            lhsT_scale=w_scales[:, w_cols],
                            rhs=x_codes[b][:, x_cols].bitcast(FP8X4),
                            rhs_scale=x_scales[b][:, x_cols],
                            start=(g == 0),
                            stop=(g == G - 1),
                        )
                nc.vector.tensor_tensor(
                    out=q_grouped[b][:, BANK * r : BANK * (r + 1)].rearrange("c (w t) -> c w t", t=PACK),
                    in0=bank[:].rearrange("c (t w) -> c w t", t=PACK),
                    in1=bias[:].unsqueeze(1).to_broadcast([P, P, PACK]),
                    op=ALU.add,
                )
                if r == R // 2:
                    quantise_q(b, 0)
            quantise_k(b)
            quantise_q(b, 1)

        def scores(b):
            shifted[b] = work.tile([P, R, WIN], F32, name="shifted")
            neg_max[b] = work.tile([P, R], F32, name="neg_max")
            for pair in range(R // 2):
                bank = psum.tile([P, BANK], F32, name="bank")
                for side in range(2):
                    r = 2 * pair + side
                    nc.tensor.matmul_mx(
                        out=bank[:, N_SCORES * side : N_SCORES * (side + 1)],
                        lhsT=q_codes[b][:, P * r : P * (r + 1)].bitcast(FP8X4),
                        lhsT_scale=q_scales[b][:, P * r : P * (r + 1)],
                        rhs=k_codes[b % 2][:, P * r : P * r + N_SCORES].bitcast(FP8X4),
                        rhs_scale=k_scales[b % 2][:, P * r : P * r + N_SCORES],
                        start=True,
                        stop=True,
                    )
                nc.vector.scalar_tensor_tensor(
                    out=shifted[b][:, 2 * pair : 2 * pair + 2, :],
                    in0=bank[:].rearrange("p (side v) -> p side v", side=2)[:, :, WIN_START : WIN_START + WIN],
                    scalar=1.0 / math.sqrt(E),
                    in1=mask[:, 2 * pair : 2 * pair + 2, :],
                    op0=ALU.mult,
                    op1=ALU.add,
                )
            for pair in range(R // 2):
                nc.vector.tensor_reduce(
                    out=neg_max[b][:, 2 * pair : 2 * pair + 2], in_=shifted[b][:, 2 * pair : 2 * pair + 2, :],
                    axis=AXIS.X, op=ALU.max, negate=True,
                )

        def exponentials(b):
            expd[b] = work.tile([P, R, WIN], F32, name="expd")
            sums[b] = work.tile([P, R], F32, name="sums")
            for r in range(R):
                nc.scalar.activation(
                    out=expd[b][:, r, :], in_=shifted[b][:, r, :], func=ACT.Exp,
                    bias=neg_max[b][:, r : r + 1], scale=1.0, accum_out=sums[b][:, r : r + 1],
                )

        def invert_sums(b):
            inv_sums[b] = work.tile([P, R], F32, name="inv_sums")
            nc.vector.reciprocal(out=inv_sums[b][:], in_=sums[b][:])

        def normalise_and_store(b):
            for r in range(R):
                row = OUT_PAD + S * r
                band = row + P * r - HALF
                nc.scalar.activation(
                    out=out_tiles[b % OUT_HOMES][:, band : band + WIN], in_=expd[b][:, r, :], func=ACT.Copy,
                    scale=inv_sums[b][:, r : r + 1],
                )
                nc.sync.dma_start(
                    out=out[b, P * r : P * (r + 1), :], in_=out_tiles[b % OUT_HOMES][:, row : row + S]
                )

        w_grouped = const.tile([P, PACK * D], BF16, name="w_grouped", align_bytes=64)
        w_codes = const.tile([P, PACK * G * P], U32, name="w_codes", align_bytes=64)
        w_scales = const.tile([P, PACK * G * P], U8, name="w_scales", align_bytes=64)
        new_x(0)
        new_x_codes(0)
        head_copies = (nc.vector.tensor_copy, nc.scalar.copy)
        for src, grouped, codes, scales in (
            (w_in, w_grouped, w_codes, w_scales),
            (x_in[0], x_grouped[0], x_codes[0], x_scales[0]),
        ):
            for n in range(W_BANKS):
                regroup_bank(src, grouped, n, head_copies[n % 2])
                if n % 2 == 1:
                    quantise_two_banks(grouped, codes, scales, n // 2)
        transpose_k(0)
        project_and_quantise(0)

        x_transposed = 1
        for i in range(B):
            if i >= 1:
                invert_sums(i - 1)
            x_wanted = min(i + 1 + min(i + 1, X_LEAD), B)
            for b in range(x_transposed, x_wanted):
                transpose_x(b)
            x_transposed = x_wanted
            if i + 1 < B:
                transpose_k(i + 1)
                quantise_x(i + 1)
            scores(i)
            if i >= 1:
                normalise_and_store(i - 1)
            exponentials(i)
            if i + 1 < B:
                project_and_quantise(i + 1)
        invert_sums(B - 1)
        normalise_and_store(B - 1)
